import numpy as np
import ml_dtypes


def mxq(x, axis, fmt="e4m3"):
    dtype, down = {"e4m3": (ml_dtypes.float8_e4m3fn, 7), "e5m2": (ml_dtypes.float8_e5m2, 14)}[fmt]
    v = np.moveaxis(np.asarray(x, np.float32).astype(ml_dtypes.bfloat16).astype(np.float64), axis, -1)
    blocks = v.reshape(v.shape[:-1] + (-1, 32))
    amax = np.abs(blocks).max(-1, keepdims=True)
    byte = np.maximum(np.where(amax > 0, np.frexp(amax)[1] - 1 + 127, 0) - down, 1)
    scale = np.exp2(byte - 127.0)
    codes = (blocks / scale).astype(np.float32).astype(dtype).astype(np.float64)
    return np.moveaxis((codes * scale).reshape(v.shape), -1, axis)


WIDE = False


def mx_kscale(k):
    if not WIDE:
        return np.ones(k)
    levels = np.array([20, -20, 10, -10, 0])
    a = np.random.permutation(np.resize(levels, k // 512 * 4)).reshape(k // 512, 4)
    idx = np.arange(k)
    return np.exp2(a[idx // 512, idx % 128 // 32])


BF16 = ml_dtypes.bfloat16


def bf(x):
    return np.asarray(x, np.float32).astype(BF16)


def f64(x):
    return np.asarray(x).astype(np.float64)


B, D, U, G = 4096, 512, 1, 8


def band_mask(input_dim, units_per_sublayer, graph_distance):
    rows = np.arange(input_dim)[:, None]
    col_block = np.arange(input_dim * units_per_sublayer) // units_per_sublayer
    m = (rows >= col_block) & (rows <= col_block + graph_distance)
    return m.astype(np.float64)


def setup_inputs():
    u = mx_kscale(D * U)
    x = bf(np.random.standard_normal((B, D)))
    W0 = bf(np.random.standard_normal((D, D * U)) * 0.8 / np.sqrt(G + 1))
    b = bf(np.random.standard_normal(D * U) * 0.1)
    g = bf(np.random.standard_normal((B, D * U)) * np.exp2(np.random.randint(-12, 1, (B, 1))) * 8.0 * u)
    z = f64(x) @ (f64(W0) * band_mask(D, U, G)) + f64(b)
    return {"x": x, "W": bf(f64(W0) / u), "b": b,
            "units_per_sublayer": U, "graph_distance": G,
            "z": np.asarray(z, np.float32), "grad_out": g}


def reference(x, W, b, units_per_sublayer, graph_distance, z, grad_out):
    Wf = f64(W)
    mask = band_mask(Wf.shape[0], units_per_sublayer, graph_distance)
    t = np.tanh(f64(z))
    dz = f64(grad_out) * (1.0 - t * t)
    return mxq(dz, 1, "e5m2") @ mxq(Wf * mask, 1, "e4m3").T

@@ -1,0 +1,200 @@
+from contextlib import ExitStack
+
+import concourse.mybir as mybir
+from concourse.masks import make_identity
+
+F32 = mybir.dt.float32
+BF16 = mybir.dt.bfloat16
+U32 = mybir.dt.uint32
+U8 = mybir.dt.uint8
+E4M3_X4 = mybir.dt.float8_e4m3fn_x4
+E5M2_X4 = mybir.dt.float8_e5m2_x4
+ALU = mybir.AluOpType
+ACT = mybir.ActivationFunctionType
+
+P = 128
+PACK = 4
+TOKENS = 4096
+FEATURES = 512
+CHUNK_TILES = 4
+CHUNKS = TOKENS // (P * CHUNK_TILES)
+PAIR = 2
+PAIR_TOKENS = PAIR * P
+PAIRS = TOKENS // PAIR_TOKENS
+PAIRS_PER_CHUNK = CHUNK_TILES // PAIR
+GPSIMD_TOKENS = 128
+DZ_LAG = 1
+OUT_LAG = 3
+
+FLOPS = 2 * TOKENS * FEATURES * FEATURES
+BYTES = TOKENS * FEATURES * (4 + 2 + 4) + FEATURES * FEATURES * 2
+
+
+def tile_compositional_t_v_kernel(
+    tc, x, W, b, units_per_sublayer, graph_distance, z, grad_out, out
+):
+    nc = tc.nc
+    assert units_per_sublayer == 1
+
+    z_chunks = z.rearrange("(c p i) j -> c p i j", p=P, i=CHUNK_TILES)
+    g_chunks = grad_out.rearrange("(c p i) j -> c p i j", p=P, i=CHUNK_TILES)
+    out_chunks = out.rearrange("(c p i) r -> c p i r", p=P, i=CHUNK_TILES)
+
+    with ExitStack() as ctx:
+        ctx.enter_context(tc.manual_schedule())
+        const = ctx.enter_context(tc.tile_pool(name="const", bufs=1))
+        loads = ctx.enter_context(tc.tile_pool(name="loads", bufs=CHUNKS))
+        stores = ctx.enter_context(tc.tile_pool(name="stores", bufs=PAIRS))
+        work = ctx.enter_context(tc.tile_pool(name="work", bufs=3))
+        psum = ctx.enter_context(tc.psum_pool(name="psum", bufs=2))
+
+        w_rows = const.tile([P, PACK, FEATURES], BF16)
+        nc.sync.dma_start(out=w_rows[:], in_=W.rearrange("(R p) j -> p R j", p=P))
+        z_sb = []
+        g_sb = []
+        for c in range(CHUNKS):
+            z_c = loads.tile([P, CHUNK_TILES, FEATURES], F32, tag="z", name="z_c")
+            nc.sync.dma_start(out=z_c[:], in_=z_chunks[c])
+            z_sb.append(z_c)
+            g_c = loads.tile([P, CHUNK_TILES, FEATURES], BF16, tag="g", name="g_c")
+            nc.sync.dma_start(out=g_c[:], in_=g_chunks[c])
+            g_sb.append(g_c)
+
+        ident_bf16 = const.tile([P, P], BF16)
+        make_identity(nc, ident_bf16[:])
+        ident_f32 = const.tile([P, P], F32)
+        make_identity(nc, ident_f32[:])
+
+        band = const.tile([P, 2 * P], F32)
+        nc.vector.memset(band[:], 1.0)
+        nc.gpsimd.affine_select(
+            out=band[:], in_=band[:], compare_op=ALU.is_ge, fill=0.0,
+            pattern=[[1, 2 * P]], base=0, channel_multiplier=-1,
+        )
+        nc.gpsimd.affine_select(
+            out=band[:], in_=band[:], compare_op=ALU.is_ge, fill=0.0,
+            pattern=[[-1, 2 * P]], base=graph_distance, channel_multiplier=1,
+        )
+
+        w_packed = const.tile([P, FEATURES, PACK], BF16, align_bytes=64)
+        w_codes = const.tile([P, FEATURES], U32, align_bytes=64)
+        w_scales = const.tile([P, FEATURES], U8, align_bytes=64)
+        nc.vector.memset(w_packed[:], 0.0)
+        wT = psum.tile([P, PACK, 2 * P], BF16, tag="gT", name="wT")
+        for t in range(PACK):
+            for R in range(t, min(t + 2, PACK)):
+                nc.tensor.transpose(
+                    wT[:, t, (R - t) * P : (R - t + 1) * P], w_rows[:, R, t * P : (t + 1) * P], ident_bf16[:]
+                )
+        for t in range(PACK):
+            rows = min(2 * P, FEATURES - t * P)
+            nc.vector.tensor_tensor(
+                out=w_packed[:, t * P : t * P + rows, t], in0=wT[:, t, :rows], in1=band[:, :rows], op=ALU.mult
+            )
+        nc.vector.quantize_mx(
+            out=w_codes[:].bitcast(E4M3_X4),
+            scales=w_scales[:],
+            in_=w_packed[:].rearrange("p r t -> p (r t)"),
+        )
+
+        zT, gT, th, sq, dz, dz_codes, dz_scales, acc, out_sb = {}, {}, {}, {}, {}, {}, {}, {}, {}
+
+        def where(n):
+            return n // PAIRS_PER_CHUNK, (n % PAIRS_PER_CHUNK) * PAIR
+
+        def transpose_z(n):
+            c, first = where(n)
+            for s in range(PAIR):
+                zT[n, s] = psum.tile([P, PACK, P], F32, tag="zT", bufs=2 * PAIR, name="zT_s")
+                for t in range(PACK):
+                    nc.tensor.transpose(
+                        zT[n, s][:, t, :], z_sb[c][:, first + s, t * P : (t + 1) * P], ident_f32[:]
+                    )
+
+        def transpose_g(n):
+            c, first = where(n)
+            gT[n] = psum.tile([P, PACK, PAIR_TOKENS], BF16, tag="gT", name="gT_n")
+            for s in range(PAIR):
+                for t in range(PACK):
+                    nc.tensor.transpose(
+                        gT[n][:, t, s * P : (s + 1) * P], g_sb[c][:, first + s, t * P : (t + 1) * P], ident_bf16[:]
+                    )
+
+        def tanh(n):
+            th[n] = work.tile([P, PAIR_TOKENS, PACK], F32, tag="th", name="th_n")
+            sq[n] = work.tile([P, PAIR_TOKENS, PACK], F32, tag="sq", name="sq_n")
+            for s in range(PAIR):
+                nc.scalar.activation(
+                    out=th[n][:, s * P : (s + 1) * P, :],
+                    in_=zT[n, s][:].rearrange("p t k -> p k t"),
+                    func=ACT.Tanh,
+                )
+                lo, hi = s * P, min((s + 1) * P, GPSIMD_TOKENS)
+                if lo < hi:
+                    nc.gpsimd.tensor_tensor(
+                        out=sq[n][:, lo:hi, :], in0=th[n][:, lo:hi, :], in1=th[n][:, lo:hi, :], op=ALU.mult
+                    )
+
+        def square_rest(n):
+            nc.scalar.activation(
+                out=sq[n][:, GPSIMD_TOKENS:, :], in_=th[n][:, GPSIMD_TOKENS:, :], func=ACT.Square
+            )
+
+        def minus_dz(n):
+            dz[n] = work.tile([P, PAIR_TOKENS, PACK], BF16, tag="dz", name="dz_n", align_bytes=64)
+            nc.vector.scalar_tensor_tensor(
+                out=dz[n][:],
+                in0=sq[n][:],
+                scalar=1.0,
+                in1=gT[n][:].rearrange("p t k -> p k t"),
+                op0=ALU.subtract,
+                op1=ALU.mult,
+            )
+
+        def quantise(n):
+            dz_codes[n] = work.tile([P, PAIR_TOKENS], U32, tag="dzc", name="dz_codes_n", align_bytes=64)
+            dz_scales[n] = work.tile([P, PAIR_TOKENS], U8, tag="dzs", name="dz_scales_n", align_bytes=64)
+            nc.vector.quantize_mx(
+                out=dz_codes[n][:].bitcast(E5M2_X4),
+                scales=dz_scales[n][:],
+                in_=dz[n][:].rearrange("p k t -> p (k t)"),
+            )
+
+        def matmuls(n):
+            for s in range(PAIR):
+                acc[n, s] = psum.tile([P, FEATURES], F32, tag="acc", name="acc_s")
+                nc.tensor.matmul_mx(
+                    out=acc[n, s][:],
+                    lhsT=dz_codes[n][:, s * P : (s + 1) * P].bitcast(E5M2_X4),
+                    lhsT_scale=dz_scales[n][:, s * P : (s + 1) * P],
+                    rhs=w_codes[:].bitcast(E4M3_X4),
+                    rhs_scale=w_scales[:],
+                    start=True,
+                    stop=True,
+                )
+
+        def store(n):
+            c, first = where(n)
+            nc.sync.dma_start(out=out_chunks[c][:, first : first + PAIR, :], in_=out_sb[n][:])
+
+        for n in range(PAIRS + OUT_LAG):
+            n_dz = n - DZ_LAG
+            n_out = n - OUT_LAG
+            if n < PAIRS:
+                transpose_z(n)
+                tanh(n)
+            if 0 <= n_dz < PAIRS:
+                transpose_g(n_dz)
+            if 0 <= n_out:
+                matmuls(n_out)
+                out_sb[n_out] = stores.tile([P, PAIR, FEATURES], F32, tag="out", name="out_n")
+                nc.scalar.mul(out=out_sb[n_out][:, 0, :], in_=acc[n_out, 0][:], mul=-1.0)
+            if n < PAIRS:
+                square_rest(n)
+            if 0 <= n_dz < PAIRS:
+                minus_dz(n_dz)
+            if 0 <= n_out:
+                nc.vector.tensor_scalar_mul(out=out_sb[n_out][:, 1, :], in0=acc[n_out, 1][:], scalar1=-1.0)
+                store(n_out)
+            if 0 <= n_dz < PAIRS:
+                quantise(n_dz)

@@ -16,13 +16,14 @@ P = 128
 PACK = 4
 TOKENS = 4096
 FEATURES = 512
-CHUNK_TILES = 4
+CHUNK_TILES = 8
 CHUNKS = TOKENS // (P * CHUNK_TILES)
 PAIR = 2
 PAIR_TOKENS = PAIR * P
 PAIRS = TOKENS // PAIR_TOKENS
 PAIRS_PER_CHUNK = CHUNK_TILES // PAIR
-GPSIMD_TOKENS = 128
+STORE_PAIRS = 2
+GPSIMD_TOKENS = 192
 DZ_LAG = 1
 OUT_LAG = 3
 
@@ -44,20 +45,26 @@ def tile_compositional_t_v_kernel(
         ctx.enter_context(tc.manual_schedule())
         const = ctx.enter_context(tc.tile_pool(name="const", bufs=1))
         loads = ctx.enter_context(tc.tile_pool(name="loads", bufs=CHUNKS))
-        stores = ctx.enter_context(tc.tile_pool(name="stores", bufs=PAIRS))
+        stores = ctx.enter_context(tc.tile_pool(name="stores", bufs=PAIRS // STORE_PAIRS))
         work = ctx.enter_context(tc.tile_pool(name="work", bufs=3))
         psum = ctx.enter_context(tc.psum_pool(name="psum", bufs=2))
 
-        w_rows = const.tile([P, PACK, FEATURES], BF16)
-        nc.sync.dma_start(out=w_rows[:], in_=W.rearrange("(R p) j -> p R j", p=P))
+        w_win = const.tile([P, PACK, 2 * P], BF16)
+        for R in range(PACK):
+            e0 = P if R == 0 else 0
+            nc.sync.dma_start(
+                out=w_win[:, R, e0:], in_=W[R * P : (R + 1) * P, (R - 1) * P + e0 : (R + 1) * P]
+            )
         z_sb = []
         g_sb = []
         for c in range(CHUNKS):
             z_c = loads.tile([P, CHUNK_TILES, FEATURES], F32, tag="z", name="z_c")
-            nc.sync.dma_start(out=z_c[:], in_=z_chunks[c])
-            z_sb.append(z_c)
             g_c = loads.tile([P, CHUNK_TILES, FEATURES], BF16, tag="g", name="g_c")
-            nc.sync.dma_start(out=g_c[:], in_=g_chunks[c])
+            piece = PAIR if c == 0 else CHUNK_TILES
+            for i in range(0, CHUNK_TILES, piece):
+                nc.sync.dma_start(out=z_c[:, i : i + piece, :], in_=z_chunks[c][:, i : i + piece, :])
+                nc.sync.dma_start(out=g_c[:, i : i + piece, :], in_=g_chunks[c][:, i : i + piece, :])
+            z_sb.append(z_c)
             g_sb.append(g_c)
 
         ident_bf16 = const.tile([P, P], BF16)
@@ -65,15 +72,16 @@ def tile_compositional_t_v_kernel(
         ident_f32 = const.tile([P, P], F32)
         make_identity(nc, ident_f32[:])
 
-        band = const.tile([P, 2 * P], F32)
+        band_rows = P + graph_distance
+        band = const.tile([P, band_rows], F32)
         nc.vector.memset(band[:], 1.0)
         nc.gpsimd.affine_select(
             out=band[:], in_=band[:], compare_op=ALU.is_ge, fill=0.0,
-            pattern=[[1, 2 * P]], base=0, channel_multiplier=-1,
+            pattern=[[1, band_rows]], base=0, channel_multiplier=-1,
         )
         nc.gpsimd.affine_select(
             out=band[:], in_=band[:], compare_op=ALU.is_ge, fill=0.0,
-            pattern=[[-1, 2 * P]], base=graph_distance, channel_multiplier=1,
+            pattern=[[-1, band_rows]], base=graph_distance, channel_multiplier=1,
         )
 
         w_packed = const.tile([P, FEATURES, PACK], BF16, align_bytes=64)
@@ -83,11 +91,12 @@ def tile_compositional_t_v_kernel(
         wT = psum.tile([P, PACK, 2 * P], BF16, tag="gT", name="wT")
         for t in range(PACK):
             for R in range(t, min(t + 2, PACK)):
+                e0 = (t - R + 1) * P
                 nc.tensor.transpose(
-                    wT[:, t, (R - t) * P : (R - t + 1) * P], w_rows[:, R, t * P : (t + 1) * P], ident_bf16[:]
+                    wT[:, t, (R - t) * P : (R - t + 1) * P], w_win[:, R, e0 : e0 + P], ident_bf16[:]
                 )
         for t in range(PACK):
-            rows = min(2 * P, FEATURES - t * P)
+            rows = min(band_rows, FEATURES - t * P)
             nc.vector.tensor_tensor(
                 out=w_packed[:, t * P : t * P + rows, t], in0=wT[:, t, :rows], in1=band[:, :rows], op=ALU.mult
             )
@@ -173,9 +182,23 @@ def tile_compositional_t_v_kernel(
                     stop=True,
                 )
 
+        def out_rows(n, s):
+            if n % STORE_PAIRS == 0 and s == 0:
+                out_sb[n // STORE_PAIRS] = stores.tile([P, STORE_PAIRS * PAIR, FEATURES], F32, tag="out", name="out_k")
+            return out_sb[n // STORE_PAIRS][:, (n % STORE_PAIRS) * PAIR + s, :]
+
         def store(n):
             c, first = where(n)
-            nc.sync.dma_start(out=out_chunks[c][:, first : first + PAIR, :], in_=out_sb[n][:])
+            if n >= PAIRS - STORE_PAIRS:
+                i = (n % STORE_PAIRS) * PAIR
+                nc.sync.dma_start(
+                    out=out_chunks[c][:, first : first + PAIR, :], in_=out_sb[n // STORE_PAIRS][:, i : i + PAIR, :]
+                )
+            elif n % STORE_PAIRS == STORE_PAIRS - 1:
+                tiles = STORE_PAIRS * PAIR
+                nc.sync.dma_start(
+                    out=out_chunks[c][:, first + PAIR - tiles : first + PAIR, :], in_=out_sb[n // STORE_PAIRS][:]
+                )
 
         for n in range(PAIRS + OUT_LAG):
             n_dz = n - DZ_LAG
@@ -187,14 +210,13 @@ def tile_compositional_t_v_kernel(
                 transpose_g(n_dz)
             if 0 <= n_out:
                 matmuls(n_out)
-                out_sb[n_out] = stores.tile([P, PAIR, FEATURES], F32, tag="out", name="out_n")
-                nc.scalar.mul(out=out_sb[n_out][:, 0, :], in_=acc[n_out, 0][:], mul=-1.0)
+                nc.scalar.mul(out=out_rows(n_out, 0), in_=acc[n_out, 0][:], mul=-1.0)
             if n < PAIRS:
                 square_rest(n)
             if 0 <= n_dz < PAIRS:
                 minus_dz(n_dz)
             if 0 <= n_out:
-                nc.vector.tensor_scalar_mul(out=out_sb[n_out][:, 1, :], in0=acc[n_out, 1][:], scalar1=-1.0)
+                nc.vector.tensor_scalar_mul(out=out_rows(n_out, 1), in0=acc[n_out, 1][:], scalar1=-1.0)
                 store(n_out)
             if 0 <= n_dz < PAIRS:
                 quantise(n_dz)

@@ -16,14 +16,12 @@ P = 128
 PACK = 4
 TOKENS = 4096
 FEATURES = 512
-CHUNK_TILES = 8
-CHUNKS = TOKENS // (P * CHUNK_TILES)
 PAIR = 2
 PAIR_TOKENS = PAIR * P
 PAIRS = TOKENS // PAIR_TOKENS
-PAIRS_PER_CHUNK = CHUNK_TILES // PAIR
-STORE_PAIRS = 2
-GPSIMD_TOKENS = 192
+CHUNK_TILES = 4
+CHUNKS = TOKENS // (P * CHUNK_TILES)
+CHUNK_PAIRS = CHUNK_TILES // PAIR
 DZ_LAG = 1
 OUT_LAG = 3
 
@@ -44,10 +42,9 @@ def tile_compositional_t_v_kernel(
     with ExitStack() as ctx:
         ctx.enter_context(tc.manual_schedule())
         const = ctx.enter_context(tc.tile_pool(name="const", bufs=1))
-        loads = ctx.enter_context(tc.tile_pool(name="loads", bufs=CHUNKS))
-        stores = ctx.enter_context(tc.tile_pool(name="stores", bufs=PAIRS // STORE_PAIRS))
+        resident = ctx.enter_context(tc.tile_pool(name="resident", bufs=CHUNKS))
         work = ctx.enter_context(tc.tile_pool(name="work", bufs=3))
-        psum = ctx.enter_context(tc.psum_pool(name="psum", bufs=2))
+        psum = ctx.enter_context(tc.psum_pool(name="psum", bufs=3))
 
         w_win = const.tile([P, PACK, 2 * P], BF16)
         for R in range(PACK):
@@ -58,8 +55,8 @@ def tile_compositional_t_v_kernel(
         z_sb = []
         g_sb = []
         for c in range(CHUNKS):
-            z_c = loads.tile([P, CHUNK_TILES, FEATURES], F32, tag="z", name="z_c")
-            g_c = loads.tile([P, CHUNK_TILES, FEATURES], BF16, tag="g", name="g_c")
+            z_c = resident.tile([P, CHUNK_TILES, FEATURES], F32, tag="z", name="z_c")
+            g_c = resident.tile([P, CHUNK_TILES, FEATURES], BF16, tag="g", name="g_c")
             piece = PAIR if c == 0 else CHUNK_TILES
             for i in range(0, CHUNK_TILES, piece):
                 nc.sync.dma_start(out=z_c[:, i : i + piece, :], in_=z_chunks[c][:, i : i + piece, :])
@@ -88,7 +85,7 @@ def tile_compositional_t_v_kernel(
         w_codes = const.tile([P, FEATURES], U32, align_bytes=64)
         w_scales = const.tile([P, FEATURES], U8, align_bytes=64)
         nc.vector.memset(w_packed[:], 0.0)
-        wT = psum.tile([P, PACK, 2 * P], BF16, tag="gT", name="wT")
+        wT = psum.tile([P, PACK, 2 * P], BF16, tag="gT", bufs=2, name="wT")
         for t in range(PACK):
             for R in range(t, min(t + 2, PACK)):
                 e0 = (t - R + 1) * P
@@ -109,12 +106,12 @@ def tile_compositional_t_v_kernel(
         zT, gT, th, sq, dz, dz_codes, dz_scales, acc, out_sb = {}, {}, {}, {}, {}, {}, {}, {}, {}
 
         def where(n):
-            return n // PAIRS_PER_CHUNK, (n % PAIRS_PER_CHUNK) * PAIR
+            return n // CHUNK_PAIRS, (n % CHUNK_PAIRS) * PAIR
 
         def transpose_z(n):
             c, first = where(n)
             for s in range(PAIR):
-                zT[n, s] = psum.tile([P, PACK, P], F32, tag="zT", bufs=2 * PAIR, name="zT_s")
+                zT[n, s] = psum.tile([P, PACK, P], F32, tag="zT", name="zT_s")
                 for t in range(PACK):
                     nc.tensor.transpose(
                         zT[n, s][:, t, :], z_sb[c][:, first + s, t * P : (t + 1) * P], ident_f32[:]
@@ -122,32 +119,27 @@ def tile_compositional_t_v_kernel(
 
         def transpose_g(n):
             c, first = where(n)
-            gT[n] = psum.tile([P, PACK, PAIR_TOKENS], BF16, tag="gT", name="gT_n")
+            gT[n] = psum.tile([P, PACK, PAIR_TOKENS], BF16, tag="gT", bufs=2, name="gT_n")
             for s in range(PAIR):
                 for t in range(PACK):
                     nc.tensor.transpose(
                         gT[n][:, t, s * P : (s + 1) * P], g_sb[c][:, first + s, t * P : (t + 1) * P], ident_bf16[:]
                     )
 
-        def tanh(n):
-            th[n] = work.tile([P, PAIR_TOKENS, PACK], F32, tag="th", name="th_n")
-            sq[n] = work.tile([P, PAIR_TOKENS, PACK], F32, tag="sq", name="sq_n")
-            for s in range(PAIR):
-                nc.scalar.activation(
-                    out=th[n][:, s * P : (s + 1) * P, :],
-                    in_=zT[n, s][:].rearrange("p t k -> p k t"),
-                    func=ACT.Tanh,
-                )
-                lo, hi = s * P, min((s + 1) * P, GPSIMD_TOKENS)
-                if lo < hi:
-                    nc.gpsimd.tensor_tensor(
-                        out=sq[n][:, lo:hi, :], in0=th[n][:, lo:hi, :], in1=th[n][:, lo:hi, :], op=ALU.mult
-                    )
-
-        def square_rest(n):
+        def tanh(n, s):
             nc.scalar.activation(
-                out=sq[n][:, GPSIMD_TOKENS:, :], in_=th[n][:, GPSIMD_TOKENS:, :], func=ACT.Square
+                out=th[n][:, s * P : (s + 1) * P, :], in_=zT[n, s][:].rearrange("p t k -> p k t"), func=ACT.Tanh
             )
+
+        def square_on_gpsimd(n, s):
+            tile_s = slice(s * P, (s + 1) * P)
+            nc.gpsimd.tensor_tensor(
+                out=sq[n][:, tile_s, :], in0=th[n][:, tile_s, :], in1=th[n][:, tile_s, :], op=ALU.mult
+            )
+
+        def square_on_scalar(n, s):
+            tile_s = slice(s * P, (s + 1) * P)
+            nc.scalar.activation(out=sq[n][:, tile_s, :], in_=th[n][:, tile_s, :], func=ACT.Square)
 
         def minus_dz(n):
             dz[n] = work.tile([P, PAIR_TOKENS, PACK], BF16, tag="dz", name="dz_n", align_bytes=64)
@@ -182,41 +174,39 @@ def tile_compositional_t_v_kernel(
                     stop=True,
                 )
 
-        def out_rows(n, s):
-            if n % STORE_PAIRS == 0 and s == 0:
-                out_sb[n // STORE_PAIRS] = stores.tile([P, STORE_PAIRS * PAIR, FEATURES], F32, tag="out", name="out_k")
-            return out_sb[n // STORE_PAIRS][:, (n % STORE_PAIRS) * PAIR + s, :]
-
         def store(n):
             c, first = where(n)
-            if n >= PAIRS - STORE_PAIRS:
-                i = (n % STORE_PAIRS) * PAIR
+            if c == CHUNKS - 1:
                 nc.sync.dma_start(
-                    out=out_chunks[c][:, first : first + PAIR, :], in_=out_sb[n // STORE_PAIRS][:, i : i + PAIR, :]
+                    out=out_chunks[c][:, first : first + PAIR, :], in_=out_sb[c][:, first : first + PAIR, :]
                 )
-            elif n % STORE_PAIRS == STORE_PAIRS - 1:
-                tiles = STORE_PAIRS * PAIR
-                nc.sync.dma_start(
-                    out=out_chunks[c][:, first + PAIR - tiles : first + PAIR, :], in_=out_sb[n // STORE_PAIRS][:]
-                )
+            elif first + PAIR == CHUNK_TILES:
+                nc.sync.dma_start(out=out_chunks[c], in_=out_sb[c][:])
 
         for n in range(PAIRS + OUT_LAG):
             n_dz = n - DZ_LAG
             n_out = n - OUT_LAG
             if n < PAIRS:
                 transpose_z(n)
-                tanh(n)
+                th[n] = work.tile([P, PAIR_TOKENS, PACK], F32, tag="th", name="th_n")
+                sq[n] = work.tile([P, PAIR_TOKENS, PACK], F32, tag="sq", name="sq_n")
+                tanh(n, 0)
+                square_on_gpsimd(n, 0)
+                tanh(n, 1)
             if 0 <= n_dz < PAIRS:
                 transpose_g(n_dz)
             if 0 <= n_out:
                 matmuls(n_out)
-                nc.scalar.mul(out=out_rows(n_out, 0), in_=acc[n_out, 0][:], mul=-1.0)
+                c, first = where(n_out)
+                if first == 0:
+                    out_sb[c] = resident.tile([P, CHUNK_TILES, FEATURES], F32, tag="out", name="out_c")
+                nc.scalar.mul(out=out_sb[c][:, first, :], in_=acc[n_out, 0][:], mul=-1.0)
             if n < PAIRS:
-                square_rest(n)
+                square_on_scalar(n, 1)
             if 0 <= n_dz < PAIRS:
                 minus_dz(n_dz)
             if 0 <= n_out:
-                nc.vector.tensor_scalar_mul(out=out_rows(n_out, 1), in0=acc[n_out, 1][:], scalar1=-1.0)
+                nc.vector.tensor_scalar_mul(out=out_sb[c][:, first + 1, :], in0=acc[n_out, 1][:], scalar1=-1.0)
                 store(n_out)
             if 0 <= n_dz < PAIRS:
                 quantise(n_dz)

@@ -22,6 +22,7 @@ PAIRS = TOKENS // PAIR_TOKENS
 CHUNK_TILES = 4
 CHUNKS = TOKENS // (P * CHUNK_TILES)
 CHUNK_PAIRS = CHUNK_TILES // PAIR
+FINE_CHUNKS = 2
 DZ_LAG = 1
 OUT_LAG = 3
 
@@ -57,7 +58,7 @@ def tile_compositional_t_v_kernel(
         for c in range(CHUNKS):
             z_c = resident.tile([P, CHUNK_TILES, FEATURES], F32, tag="z", name="z_c")
             g_c = resident.tile([P, CHUNK_TILES, FEATURES], BF16, tag="g", name="g_c")
-            piece = PAIR if c == 0 else CHUNK_TILES
+            piece = PAIR if c < FINE_CHUNKS else CHUNK_TILES
             for i in range(0, CHUNK_TILES, piece):
                 nc.sync.dma_start(out=z_c[:, i : i + piece, :], in_=z_chunks[c][:, i : i + piece, :])
                 nc.sync.dma_start(out=g_c[:, i : i + piece, :], in_=g_chunks[c][:, i : i + piece, :])
@@ -71,7 +72,7 @@ def tile_compositional_t_v_kernel(
 
         band_rows = P + graph_distance
         band = const.tile([P, band_rows], F32)
-        nc.vector.memset(band[:], 1.0)
+        nc.vector.memset(band[:], -1.0)
         nc.gpsimd.affine_select(
             out=band[:], in_=band[:], compare_op=ALU.is_ge, fill=0.0,
             pattern=[[1, band_rows]], base=0, channel_multiplier=-1,
@@ -174,6 +175,14 @@ def tile_compositional_t_v_kernel(
                     stop=True,
                 )
 
+        def copy_on_scalar(n, s):
+            c, first = where(n)
+            nc.scalar.copy(out=out_sb[c][:, first + s, :], in_=acc[n, s][:])
+
+        def copy_on_vector(n, s):
+            c, first = where(n)
+            nc.vector.tensor_copy(out=out_sb[c][:, first + s, :], in_=acc[n, s][:])
+
         def store(n):
             c, first = where(n)
             if c == CHUNKS - 1:
@@ -186,6 +195,7 @@ def tile_compositional_t_v_kernel(
         for n in range(PAIRS + OUT_LAG):
             n_dz = n - DZ_LAG
             n_out = n - OUT_LAG
+            both_on_scalar = n >= PAIRS and n_out < PAIRS - 1
             if n < PAIRS:
                 transpose_z(n)
                 th[n] = work.tile([P, PAIR_TOKENS, PACK], F32, tag="th", name="th_n")
@@ -193,20 +203,22 @@ def tile_compositional_t_v_kernel(
                 tanh(n, 0)
                 square_on_gpsimd(n, 0)
                 tanh(n, 1)
-            if 0 <= n_dz < PAIRS:
-                transpose_g(n_dz)
             if 0 <= n_out:
                 matmuls(n_out)
                 c, first = where(n_out)
                 if first == 0:
                     out_sb[c] = resident.tile([P, CHUNK_TILES, FEATURES], F32, tag="out", name="out_c")
-                nc.scalar.mul(out=out_sb[c][:, first, :], in_=acc[n_out, 0][:], mul=-1.0)
+                copy_on_scalar(n_out, 0)
+                if both_on_scalar:
+                    copy_on_scalar(n_out, 1)
             if n < PAIRS:
+                transpose_g(n)
                 square_on_scalar(n, 1)
             if 0 <= n_dz < PAIRS:
                 minus_dz(n_dz)
             if 0 <= n_out:
-                nc.vector.tensor_scalar_mul(out=out_sb[c][:, first + 1, :], in0=acc[n_out, 1][:], scalar1=-1.0)
+                if not both_on_scalar:
+                    copy_on_vector(n_out, 1)
                 store(n_out)
             if 0 <= n_dz < PAIRS:
                 quantise(n_dz)

@@ -19,10 +19,9 @@ FEATURES = 512
 PAIR = 2
 PAIR_TOKENS = PAIR * P
 PAIRS = TOKENS // PAIR_TOKENS
-CHUNK_TILES = 4
-CHUNKS = TOKENS // (P * CHUNK_TILES)
-CHUNK_PAIRS = CHUNK_TILES // PAIR
-FINE_CHUNKS = 2
+TILES = TOKENS // P
+LOADS = [("z", 1), ("g", 1), ("z", 1), ("g", 1), ("z", 2), ("g", 2), ("z", 2), ("g", 2), ("z", 4), ("g", 2), ("g", 2), ("z", 6), ("g", 3), ("g", 3)]
+STORES = [7, 3, 2, 1, 1, 1, 1]
 DZ_LAG = 1
 OUT_LAG = 3
 
@@ -36,14 +35,14 @@ def tile_compositional_t_v_kernel(
     nc = tc.nc
     assert units_per_sublayer == 1
 
-    z_chunks = z.rearrange("(c p i) j -> c p i j", p=P, i=CHUNK_TILES)
-    g_chunks = grad_out.rearrange("(c p i) j -> c p i j", p=P, i=CHUNK_TILES)
-    out_chunks = out.rearrange("(c p i) r -> c p i r", p=P, i=CHUNK_TILES)
+    z_rows = z.rearrange("(p i) j -> p i j", i=TILES)
+    g_rows = grad_out.rearrange("(p i) j -> p i j", i=TILES)
+    out_rows = out.rearrange("(p i) r -> p i r", i=TILES)
 
     with ExitStack() as ctx:
         ctx.enter_context(tc.manual_schedule())
         const = ctx.enter_context(tc.tile_pool(name="const", bufs=1))
-        resident = ctx.enter_context(tc.tile_pool(name="resident", bufs=CHUNKS))
+        resident = ctx.enter_context(tc.tile_pool(name="resident", bufs=1))
         work = ctx.enter_context(tc.tile_pool(name="work", bufs=3))
         psum = ctx.enter_context(tc.psum_pool(name="psum", bufs=3))
 
@@ -53,17 +52,16 @@ def tile_compositional_t_v_kernel(
             nc.sync.dma_start(
                 out=w_win[:, R, e0:], in_=W[R * P : (R + 1) * P, (R - 1) * P + e0 : (R + 1) * P]
             )
-        z_sb = []
-        g_sb = []
-        for c in range(CHUNKS):
-            z_c = resident.tile([P, CHUNK_TILES, FEATURES], F32, tag="z", name="z_c")
-            g_c = resident.tile([P, CHUNK_TILES, FEATURES], BF16, tag="g", name="g_c")
-            piece = PAIR if c < FINE_CHUNKS else CHUNK_TILES
-            for i in range(0, CHUNK_TILES, piece):
-                nc.sync.dma_start(out=z_c[:, i : i + piece, :], in_=z_chunks[c][:, i : i + piece, :])
-                nc.sync.dma_start(out=g_c[:, i : i + piece, :], in_=g_chunks[c][:, i : i + piece, :])
-            z_sb.append(z_c)
-            g_sb.append(g_c)
+        z_of = []
+        g_of = []
+        for kind, pairs in LOADS:
+            rows, dtype, of = (z_rows, F32, z_of) if kind == "z" else (g_rows, BF16, g_of)
+            first = len(of) * PAIR
+            piece = resident.tile(
+                [P, pairs * PAIR, FEATURES], dtype, tag="%s%d" % (kind, first), name="piece"
+            )
+            nc.sync.dma_start(out=piece[:], in_=rows[:, first : first + pairs * PAIR, :])
+            of.extend(piece[:, i * PAIR : (i + 1) * PAIR, :] for i in range(pairs))
 
         ident_bf16 = const.tile([P, P], BF16)
         make_identity(nc, ident_bf16[:])
@@ -106,25 +104,26 @@ def tile_compositional_t_v_kernel(
 
         zT, gT, th, sq, dz, dz_codes, dz_scales, acc, out_sb = {}, {}, {}, {}, {}, {}, {}, {}, {}
 
-        def where(n):
-            return n // CHUNK_PAIRS, (n % CHUNK_PAIRS) * PAIR
+        first_of, end_of = [], []
+        for pairs in STORES:
+            start = len(first_of)
+            first_of.extend([start] * pairs)
+            end_of.extend([start + pairs] * pairs)
 
         def transpose_z(n):
-            c, first = where(n)
             for s in range(PAIR):
                 zT[n, s] = psum.tile([P, PACK, P], F32, tag="zT", name="zT_s")
                 for t in range(PACK):
                     nc.tensor.transpose(
-                        zT[n, s][:, t, :], z_sb[c][:, first + s, t * P : (t + 1) * P], ident_f32[:]
+                        zT[n, s][:, t, :], z_of[n][:, s, t * P : (t + 1) * P], ident_f32[:]
                     )
 
         def transpose_g(n):
-            c, first = where(n)
             gT[n] = psum.tile([P, PACK, PAIR_TOKENS], BF16, tag="gT", bufs=2, name="gT_n")
             for s in range(PAIR):
                 for t in range(PACK):
                     nc.tensor.transpose(
-                        gT[n][:, t, s * P : (s + 1) * P], g_sb[c][:, first + s, t * P : (t + 1) * P], ident_bf16[:]
+                        gT[n][:, t, s * P : (s + 1) * P], g_of[n][:, s, t * P : (t + 1) * P], ident_bf16[:]
                     )
 
         def tanh(n, s):
@@ -175,22 +174,19 @@ def tile_compositional_t_v_kernel(
                     stop=True,
                 )
 
+        def out_tile(n, s):
+            return out_sb[first_of[n]][:, (n - first_of[n]) * PAIR + s, :]
+
         def copy_on_scalar(n, s):
-            c, first = where(n)
-            nc.scalar.copy(out=out_sb[c][:, first + s, :], in_=acc[n, s][:])
+            nc.scalar.copy(out=out_tile(n, s), in_=acc[n, s][:])
 
         def copy_on_vector(n, s):
-            c, first = where(n)
-            nc.vector.tensor_copy(out=out_sb[c][:, first + s, :], in_=acc[n, s][:])
+            nc.vector.tensor_copy(out=out_tile(n, s), in_=acc[n, s][:])
 
         def store(n):
-            c, first = where(n)
-            if c == CHUNKS - 1:
-                nc.sync.dma_start(
-                    out=out_chunks[c][:, first : first + PAIR, :], in_=out_sb[c][:, first : first + PAIR, :]
-                )
-            elif first + PAIR == CHUNK_TILES:
-                nc.sync.dma_start(out=out_chunks[c], in_=out_sb[c][:])
+            if n + 1 == end_of[n]:
+                first = first_of[n]
+                nc.sync.dma_start(out=out_rows[:, first * PAIR : (n + 1) * PAIR, :], in_=out_sb[first][:])
 
         for n in range(PAIRS + OUT_LAG):
             n_dz = n - DZ_LAG
@@ -205,9 +201,10 @@ def tile_compositional_t_v_kernel(
                 tanh(n, 1)
             if 0 <= n_out:
                 matmuls(n_out)
-                c, first = where(n_out)
-                if first == 0:
-                    out_sb[c] = resident.tile([P, CHUNK_TILES, FEATURES], F32, tag="out", name="out_c")
+                if n_out == first_of[n_out]:
+                    out_sb[n_out] = resident.tile(
+                        [P, (end_of[n_out] - n_out) * PAIR, FEATURES], F32, tag="out%d" % n_out, name="group"
+                    )
                 copy_on_scalar(n_out, 0)
                 if both_on_scalar:
                     copy_on_scalar(n_out, 1)

@@ -20,9 +20,14 @@ PAIR = 2
 PAIR_TOKENS = PAIR * P
 PAIRS = TOKENS // PAIR_TOKENS
 TILES = TOKENS // P
-LOADS = [("z", 1), ("g", 1), ("z", 1), ("g", 1), ("z", 2), ("g", 2), ("z", 2), ("g", 2), ("z", 4), ("g", 2), ("g", 2), ("z", 6), ("g", 3), ("g", 3)]
-STORES = [7, 3, 2, 1, 1, 1, 1]
+LOADS = [
+    ("z", 1), ("z", 1), ("g", 2), ("z", 2), ("g", 2), ("z", 4), ("g", 4), ("z", 4), ("g", 4), ("z", 4), ("g", 4),
+    ("z", 8), ("g", 4), ("g", 4), ("z", 8), ("g", 8),
+]
+STORES = [14, 8, 4, 2, 2, 1, 1]
+VECTOR_BOTH = 6
 DZ_LAG = 1
+LATE = [(PAIRS - 2, 0), (PAIRS - 2, 1), (PAIRS - 1, 1)]
 OUT_LAG = 3
 
 FLOPS = 2 * TOKENS * FEATURES * FEATURES
@@ -47,6 +52,7 @@ def tile_compositional_t_v_kernel(
         psum = ctx.enter_context(tc.psum_pool(name="psum", bufs=3))
 
         w_win = const.tile([P, PACK, 2 * P], BF16)
+
         for R in range(PACK):
             e0 = P if R == 0 else 0
             nc.sync.dma_start(
@@ -54,14 +60,12 @@ def tile_compositional_t_v_kernel(
             )
         z_of = []
         g_of = []
-        for kind, pairs in LOADS:
+        for kind, tiles in LOADS:
             rows, dtype, of = (z_rows, F32, z_of) if kind == "z" else (g_rows, BF16, g_of)
-            first = len(of) * PAIR
-            piece = resident.tile(
-                [P, pairs * PAIR, FEATURES], dtype, tag="%s%d" % (kind, first), name="piece"
-            )
-            nc.sync.dma_start(out=piece[:], in_=rows[:, first : first + pairs * PAIR, :])
-            of.extend(piece[:, i * PAIR : (i + 1) * PAIR, :] for i in range(pairs))
+            first = len(of)
+            piece = resident.tile([P, tiles, FEATURES], dtype, tag="%s%d" % (kind, first), name="piece")
+            nc.sync.dma_start(out=piece[:], in_=rows[:, first : first + tiles, :])
+            of.extend(piece[:, i, :] for i in range(tiles))
 
         ident_bf16 = const.tile([P, P], BF16)
         make_identity(nc, ident_bf16[:])
@@ -84,6 +88,7 @@ def tile_compositional_t_v_kernel(
         w_codes = const.tile([P, FEATURES], U32, align_bytes=64)
         w_scales = const.tile([P, FEATURES], U8, align_bytes=64)
         nc.vector.memset(w_packed[:], 0.0)
+
         wT = psum.tile([P, PACK, 2 * P], BF16, tag="gT", bufs=2, name="wT")
         for t in range(PACK):
             for R in range(t, min(t + 2, PACK)):
@@ -105,17 +110,22 @@ def tile_compositional_t_v_kernel(
         zT, gT, th, sq, dz, dz_codes, dz_scales, acc, out_sb = {}, {}, {}, {}, {}, {}, {}, {}, {}
 
         first_of, end_of = [], []
-        for pairs in STORES:
+        for tiles in STORES:
             start = len(first_of)
-            first_of.extend([start] * pairs)
-            end_of.extend([start + pairs] * pairs)
+            first_of.extend([start] * tiles)
+            end_of.extend([start + tiles] * tiles)
+
+        def parts(n):
+            if n < PAIRS - 1:
+                return [slice(0, PAIR_TOKENS)]
+            return [slice(P, PAIR_TOKENS), slice(0, P)]
 
         def transpose_z(n):
             for s in range(PAIR):
                 zT[n, s] = psum.tile([P, PACK, P], F32, tag="zT", name="zT_s")
                 for t in range(PACK):
                     nc.tensor.transpose(
-                        zT[n, s][:, t, :], z_of[n][:, s, t * P : (t + 1) * P], ident_f32[:]
+                        zT[n, s][:, t, :], z_of[n * PAIR + s][:, t * P : (t + 1) * P], ident_f32[:]
                     )
 
         def transpose_g(n):
@@ -123,7 +133,7 @@ def tile_compositional_t_v_kernel(
             for s in range(PAIR):
                 for t in range(PACK):
                     nc.tensor.transpose(
-                        gT[n][:, t, s * P : (s + 1) * P], g_of[n][:, s, t * P : (t + 1) * P], ident_bf16[:]
+                        gT[n][:, t, s * P : (s + 1) * P], g_of[n * PAIR + s][:, t * P : (t + 1) * P], ident_bf16[:]
                     )
 
         def tanh(n, s):
@@ -143,27 +153,33 @@ def tile_compositional_t_v_kernel(
 
         def minus_dz(n):
             dz[n] = work.tile([P, PAIR_TOKENS, PACK], BF16, tag="dz", name="dz_n", align_bytes=64)
-            nc.vector.scalar_tensor_tensor(
-                out=dz[n][:],
-                in0=sq[n][:],
-                scalar=1.0,
-                in1=gT[n][:].rearrange("p t k -> p k t"),
-                op0=ALU.subtract,
-                op1=ALU.mult,
-            )
+            for part in parts(n):
+                nc.vector.scalar_tensor_tensor(
+                    out=dz[n][:, part, :],
+                    in0=sq[n][:, part, :],
+                    scalar=1.0,
+                    in1=gT[n][:, :, part].rearrange("p t k -> p k t"),
+                    op0=ALU.subtract,
+                    op1=ALU.mult,
+                )
 
         def quantise(n):
             dz_codes[n] = work.tile([P, PAIR_TOKENS], U32, tag="dzc", name="dz_codes_n", align_bytes=64)
             dz_scales[n] = work.tile([P, PAIR_TOKENS], U8, tag="dzs", name="dz_scales_n", align_bytes=64)
-            nc.vector.quantize_mx(
-                out=dz_codes[n][:].bitcast(E5M2_X4),
-                scales=dz_scales[n][:],
-                in_=dz[n][:].rearrange("p k t -> p (k t)"),
-            )
+            for part in parts(n):
+                nc.vector.quantize_mx(
+                    out=dz_codes[n][:, part].bitcast(E5M2_X4),
+                    scales=dz_scales[n][:, part],
+                    in_=dz[n][:, part, :].rearrange("p k t -> p (k t)"),
+                )
+
+        def order(n):
+            return [0, 1] if n < PAIRS - 1 else [1, 0]
 
         def matmuls(n):
-            for s in range(PAIR):
-                acc[n, s] = psum.tile([P, FEATURES], F32, tag="acc", name="acc_s")
+            for s in order(n):
+                tag = "zT" if (n, s) in LATE else "acc"
+                acc[n, s] = psum.tile([P, FEATURES], F32, tag=tag, name="acc_s")
                 nc.tensor.matmul_mx(
                     out=acc[n, s][:],
                     lhsT=dz_codes[n][:, s * P : (s + 1) * P].bitcast(E5M2_X4),
@@ -175,7 +191,12 @@ def tile_compositional_t_v_kernel(
                 )
 
         def out_tile(n, s):
-            return out_sb[first_of[n]][:, (n - first_of[n]) * PAIR + s, :]
+            i = n * PAIR + s
+            if first_of[i] not in out_sb:
+                out_sb[first_of[i]] = resident.tile(
+                    [P, end_of[i] - first_of[i], FEATURES], F32, tag="out%d" % first_of[i], name="group"
+                )
+            return out_sb[first_of[i]][:, i - first_of[i], :]
 
         def copy_on_scalar(n, s):
             nc.scalar.copy(out=out_tile(n, s), in_=acc[n, s][:])
@@ -184,14 +205,16 @@ def tile_compositional_t_v_kernel(
             nc.vector.tensor_copy(out=out_tile(n, s), in_=acc[n, s][:])
 
         def store(n):
-            if n + 1 == end_of[n]:
-                first = first_of[n]
-                nc.sync.dma_start(out=out_rows[:, first * PAIR : (n + 1) * PAIR, :], in_=out_sb[first][:])
+            for s in order(n):
+                i = n * PAIR + s
+                if i + 1 == end_of[i]:
+                    nc.sync.dma_start(out=out_rows[:, first_of[i] : i + 1, :], in_=out_sb[first_of[i]][:])
 
         for n in range(PAIRS + OUT_LAG):
             n_dz = n - DZ_LAG
             n_out = n - OUT_LAG
             both_on_scalar = n >= PAIRS and n_out < PAIRS - 1
+            both_on_vector = n < PAIRS and n % VECTOR_BOTH == VECTOR_BOTH - 1
             if n < PAIRS:
                 transpose_z(n)
                 th[n] = work.tile([P, PAIR_TOKENS, PACK], F32, tag="th", name="th_n")
@@ -199,21 +222,23 @@ def tile_compositional_t_v_kernel(
                 tanh(n, 0)
                 square_on_gpsimd(n, 0)
                 tanh(n, 1)
+            if n == PAIRS - 1:
+                square_on_scalar(n, 1)
             if 0 <= n_out:
                 matmuls(n_out)
-                if n_out == first_of[n_out]:
-                    out_sb[n_out] = resident.tile(
-                        [P, (end_of[n_out] - n_out) * PAIR, FEATURES], F32, tag="out%d" % n_out, name="group"
-                    )
-                copy_on_scalar(n_out, 0)
+                if not both_on_vector:
+                    copy_on_scalar(n_out, 0)
                 if both_on_scalar:
                     copy_on_scalar(n_out, 1)
             if n < PAIRS:
                 transpose_g(n)
-                square_on_scalar(n, 1)
+                if n < PAIRS - 1:
+                    square_on_scalar(n, 1)
             if 0 <= n_dz < PAIRS:
                 minus_dz(n_dz)
             if 0 <= n_out:
+                if both_on_vector:
+                    copy_on_vector(n_out, 0)
                 if not both_on_scalar:
                     copy_on_vector(n_out, 1)
                 store(n_out)

@@ -24,8 +24,7 @@ LOADS = [
     ("z", 1), ("z", 1), ("g", 2), ("z", 2), ("g", 2), ("z", 4), ("g", 4), ("z", 4), ("g", 4), ("z", 4), ("g", 4),
     ("z", 8), ("g", 4), ("g", 4), ("z", 8), ("g", 8),
 ]
-STORES = [14, 8, 4, 2, 2, 1, 1]
-VECTOR_BOTH = 6
+STORES = [10, 4, 4, 2, 2, 2, 2, 2, 2, 1, 1]
 DZ_LAG = 1
 LATE = [(PAIRS - 2, 0), (PAIRS - 2, 1), (PAIRS - 1, 1)]
 OUT_LAG = 3
@@ -214,7 +213,6 @@ def tile_compositional_t_v_kernel(
             n_dz = n - DZ_LAG
             n_out = n - OUT_LAG
             both_on_scalar = n >= PAIRS and n_out < PAIRS - 1
-            both_on_vector = n < PAIRS and n % VECTOR_BOTH == VECTOR_BOTH - 1
             if n < PAIRS:
                 transpose_z(n)
                 th[n] = work.tile([P, PAIR_TOKENS, PACK], F32, tag="th", name="th_n")
@@ -226,8 +224,7 @@ def tile_compositional_t_v_kernel(
                 square_on_scalar(n, 1)
             if 0 <= n_out:
                 matmuls(n_out)
-                if not both_on_vector:
-                    copy_on_scalar(n_out, 0)
+                copy_on_scalar(n_out, 0)
                 if both_on_scalar:
                     copy_on_scalar(n_out, 1)
             if n < PAIRS:
@@ -237,8 +234,6 @@ def tile_compositional_t_v_kernel(
             if 0 <= n_dz < PAIRS:
                 minus_dz(n_dz)
             if 0 <= n_out:
-                if both_on_vector:
-                    copy_on_vector(n_out, 0)
                 if not both_on_scalar:
                     copy_on_vector(n_out, 1)
                 store(n_out)

from contextlib import ExitStack

import concourse.mybir as mybir
from concourse.masks import make_identity

F32 = mybir.dt.float32
BF16 = mybir.dt.bfloat16
U32 = mybir.dt.uint32
U8 = mybir.dt.uint8
E4M3_X4 = mybir.dt.float8_e4m3fn_x4
E5M2_X4 = mybir.dt.float8_e5m2_x4
ALU = mybir.AluOpType
ACT = mybir.ActivationFunctionType

P = 128
PACK = 4
TOKENS = 4096
FEATURES = 512
PAIR = 2
PAIR_TOKENS = PAIR * P
PAIRS = TOKENS // PAIR_TOKENS
TILES = TOKENS // P
LOADS = [
    ("z", 1), ("z", 1), ("g", 2), ("z", 2), ("g", 2), ("z", 4), ("g", 4), ("z", 4), ("g", 4), ("z", 4), ("g", 4),
    ("z", 8), ("g", 4), ("g", 4), ("z", 8), ("g", 8),
]
STORES = [10, 4, 4, 2, 2, 2, 2, 2, 2, 1, 1]
DZ_LAG = 1
LATE = [(PAIRS - 2, 0), (PAIRS - 2, 1), (PAIRS - 1, 1)]
OUT_LAG = 3

FLOPS = 2 * TOKENS * FEATURES * FEATURES
BYTES = TOKENS * FEATURES * (4 + 2 + 4) + FEATURES * FEATURES * 2


def tile_compositional_t_v_kernel(
    tc, x, W, b, units_per_sublayer, graph_distance, z, grad_out, out
):
    nc = tc.nc
    assert units_per_sublayer == 1

    z_rows = z.rearrange("(p i) j -> p i j", i=TILES)
    g_rows = grad_out.rearrange("(p i) j -> p i j", i=TILES)
    out_rows = out.rearrange("(p i) r -> p i r", i=TILES)

    with ExitStack() as ctx:
        ctx.enter_context(tc.manual_schedule())
        const = ctx.enter_context(tc.tile_pool(name="const", bufs=1))
        resident = ctx.enter_context(tc.tile_pool(name="resident", bufs=1))
        work = ctx.enter_context(tc.tile_pool(name="work", bufs=3))
        psum = ctx.enter_context(tc.psum_pool(name="psum", bufs=3))

        w_win = const.tile([P, PACK, 2 * P], BF16)

        for R in range(PACK):
            e0 = P if R == 0 else 0
            nc.sync.dma_start(
                out=w_win[:, R, e0:], in_=W[R * P : (R + 1) * P, (R - 1) * P + e0 : (R + 1) * P]
            )
        z_of = []
        g_of = []
        for kind, tiles in LOADS:
            rows, dtype, of = (z_rows, F32, z_of) if kind == "z" else (g_rows, BF16, g_of)
            first = len(of)
            piece = resident.tile([P, tiles, FEATURES], dtype, tag="%s%d" % (kind, first), name="piece")
            nc.sync.dma_start(out=piece[:], in_=rows[:, first : first + tiles, :])
            of.extend(piece[:, i, :] for i in range(tiles))

        ident_bf16 = const.tile([P, P], BF16)
        make_identity(nc, ident_bf16[:])
        ident_f32 = const.tile([P, P], F32)
        make_identity(nc, ident_f32[:])

        band_rows = P + graph_distance
        band = const.tile([P, band_rows], F32)
        nc.vector.memset(band[:], -1.0)
        nc.gpsimd.affine_select(
            out=band[:], in_=band[:], compare_op=ALU.is_ge, fill=0.0,
            pattern=[[1, band_rows]], base=0, channel_multiplier=-1,
        )
        nc.gpsimd.affine_select(
            out=band[:], in_=band[:], compare_op=ALU.is_ge, fill=0.0,
            pattern=[[-1, band_rows]], base=graph_distance, channel_multiplier=1,
        )

        w_packed = const.tile([P, FEATURES, PACK], BF16, align_bytes=64)
        w_codes = const.tile([P, FEATURES], U32, align_bytes=64)
        w_scales = const.tile([P, FEATURES], U8, align_bytes=64)
        nc.vector.memset(w_packed[:], 0.0)

        wT = psum.tile([P, PACK, 2 * P], BF16, tag="gT", bufs=2, name="wT")
        for t in range(PACK):
            for R in range(t, min(t + 2, PACK)):
                e0 = (t - R + 1) * P
                nc.tensor.transpose(
                    wT[:, t, (R - t) * P : (R - t + 1) * P], w_win[:, R, e0 : e0 + P], ident_bf16[:]
                )
        for t in range(PACK):
            rows = min(band_rows, FEATURES - t * P)
            nc.vector.tensor_tensor(
                out=w_packed[:, t * P : t * P + rows, t], in0=wT[:, t, :rows], in1=band[:, :rows], op=ALU.mult
            )
        nc.vector.quantize_mx(
            out=w_codes[:].bitcast(E4M3_X4),
            scales=w_scales[:],
            in_=w_packed[:].rearrange("p r t -> p (r t)"),
        )

        zT, gT, th, sq, dz, dz_codes, dz_scales, acc, out_sb = {}, {}, {}, {}, {}, {}, {}, {}, {}

        first_of, end_of = [], []
        for tiles in STORES:
            start = len(first_of)
            first_of.extend([start] * tiles)
            end_of.extend([start + tiles] * tiles)

        def parts(n):
            if n < PAIRS - 1:
                return [slice(0, PAIR_TOKENS)]
            return [slice(P, PAIR_TOKENS), slice(0, P)]

        def transpose_z(n):
            for s in range(PAIR):
                zT[n, s] = psum.tile([P, PACK, P], F32, tag="zT", name="zT_s")
                for t in range(PACK):
                    nc.tensor.transpose(
                        zT[n, s][:, t, :], z_of[n * PAIR + s][:, t * P : (t + 1) * P], ident_f32[:]
                    )

        def transpose_g(n):
            gT[n] = psum.tile([P, PACK, PAIR_TOKENS], BF16, tag="gT", bufs=2, name="gT_n")
            for s in range(PAIR):
                for t in range(PACK):
                    nc.tensor.transpose(
                        gT[n][:, t, s * P : (s + 1) * P], g_of[n * PAIR + s][:, t * P : (t + 1) * P], ident_bf16[:]
                    )

        def tanh(n, s):
            nc.scalar.activation(
                out=th[n][:, s * P : (s + 1) * P, :], in_=zT[n, s][:].rearrange("p t k -> p k t"), func=ACT.Tanh
            )

        def square_on_gpsimd(n, s):
            tile_s = slice(s * P, (s + 1) * P)
            nc.gpsimd.tensor_tensor(
                out=sq[n][:, tile_s, :], in0=th[n][:, tile_s, :], in1=th[n][:, tile_s, :], op=ALU.mult
            )

        def square_on_scalar(n, s):
            tile_s = slice(s * P, (s + 1) * P)
            nc.scalar.activation(out=sq[n][:, tile_s, :], in_=th[n][:, tile_s, :], func=ACT.Square)

        def minus_dz(n):
            dz[n] = work.tile([P, PAIR_TOKENS, PACK], BF16, tag="dz", name="dz_n", align_bytes=64)
            for part in parts(n):
                nc.vector.scalar_tensor_tensor(
                    out=dz[n][:, part, :],
                    in0=sq[n][:, part, :],
                    scalar=1.0,
                    in1=gT[n][:, :, part].rearrange("p t k -> p k t"),
                    op0=ALU.subtract,
                    op1=ALU.mult,
                )

        def quantise(n):
            dz_codes[n] = work.tile([P, PAIR_TOKENS], U32, tag="dzc", name="dz_codes_n", align_bytes=64)
            dz_scales[n] = work.tile([P, PAIR_TOKENS], U8, tag="dzs", name="dz_scales_n", align_bytes=64)
            for part in parts(n):
                nc.vector.quantize_mx(
                    out=dz_codes[n][:, part].bitcast(E5M2_X4),
                    scales=dz_scales[n][:, part],
                    in_=dz[n][:, part, :].rearrange("p k t -> p (k t)"),
                )

        def order(n):
            return [0, 1] if n < PAIRS - 1 else [1, 0]

        def matmuls(n):
            for s in order(n):
                tag = "zT" if (n, s) in LATE else "acc"
                acc[n, s] = psum.tile([P, FEATURES], F32, tag=tag, name="acc_s")
                nc.tensor.matmul_mx(
                    out=acc[n, s][:],
                    lhsT=dz_codes[n][:, s * P : (s + 1) * P].bitcast(E5M2_X4),
                    lhsT_scale=dz_scales[n][:, s * P : (s + 1) * P],
                    rhs=w_codes[:].bitcast(E4M3_X4),
                    rhs_scale=w_scales[:],
                    start=True,
                    stop=True,
                )

        def out_tile(n, s):
            i = n * PAIR + s
            if first_of[i] not in out_sb:
                out_sb[first_of[i]] = resident.tile(
                    [P, end_of[i] - first_of[i], FEATURES], F32, tag="out%d" % first_of[i], name="group"
                )
            return out_sb[first_of[i]][:, i - first_of[i], :]

        def copy_on_scalar(n, s):
            nc.scalar.copy(out=out_tile(n, s), in_=acc[n, s][:])

        def copy_on_vector(n, s):
            nc.vector.tensor_copy(out=out_tile(n, s), in_=acc[n, s][:])

        def store(n):
            for s in order(n):
                i = n * PAIR + s
                if i + 1 == end_of[i]:
                    nc.sync.dma_start(out=out_rows[:, first_of[i] : i + 1, :], in_=out_sb[first_of[i]][:])

        for n in range(PAIRS + OUT_LAG):
            n_dz = n - DZ_LAG
            n_out = n - OUT_LAG
            both_on_scalar = n >= PAIRS and n_out < PAIRS - 1
            if n < PAIRS:
                transpose_z(n)
                th[n] = work.tile([P, PAIR_TOKENS, PACK], F32, tag="th", name="th_n")
                sq[n] = work.tile([P, PAIR_TOKENS, PACK], F32, tag="sq", name="sq_n")
                tanh(n, 0)
                square_on_gpsimd(n, 0)
                tanh(n, 1)
            if n == PAIRS - 1:
                square_on_scalar(n, 1)
            if 0 <= n_out:
                matmuls(n_out)
                copy_on_scalar(n_out, 0)
                if both_on_scalar:
                    copy_on_scalar(n_out, 1)
            if n < PAIRS:
                transpose_g(n)
                if n < PAIRS - 1:
                    square_on_scalar(n, 1)
            if 0 <= n_dz < PAIRS:
                minus_dz(n_dz)
            if 0 <= n_out:
                if not both_on_scalar:
                    copy_on_vector(n_out, 1)
                store(n_out)
            if 0 <= n_dz < PAIRS:
                quantise(n_dz)
